import numpy as np
import ml_dtypes


def mxq(x, axis, fmt="e4m3"):
    dtype, down = {"e4m3": (ml_dtypes.float8_e4m3fn, 7), "e5m2": (ml_dtypes.float8_e5m2, 14)}[fmt]
    v = np.moveaxis(np.asarray(x, np.float32).astype(ml_dtypes.bfloat16).astype(np.float64), axis, -1)
    blocks = v.reshape(v.shape[:-1] + (-1, 32))
    amax = np.abs(blocks).max(-1, keepdims=True)
    byte = np.maximum(np.where(amax > 0, np.frexp(amax)[1] - 1 + 127, 0) - down, 1)
    scale = np.exp2(byte - 127.0)
    codes = (blocks / scale).astype(np.float32).astype(dtype).astype(np.float64)
    return np.moveaxis((codes * scale).reshape(v.shape), -1, axis)


WIDE = False


def mx_kscale(k):
    if not WIDE:
        return np.ones(k)
    levels = np.array([10, -10, 5, -5, 0])
    a = np.random.permutation(np.resize(levels, k // 512 * 4)).reshape(k // 512, 4)
    idx = np.arange(k)
    return np.exp2(a[idx // 512, idx % 128 // 32])


BF16 = ml_dtypes.bfloat16


def bf(x):
    return np.asarray(x, np.float32).astype(BF16)


def f64(x):
    return np.asarray(x).astype(np.float64)


B, C, D, O = 2, 256, 2048, 128
S0 = 1
S = 2
P = D // (S * (S0 + 1))
K = S * C


def setup_inputs():
    s = mx_kscale(K).reshape(S, C)
    sx = np.tile(np.repeat(s.T, S0 + 1, axis=1), (1, P))
    return {"x": bf(np.random.standard_normal((B, C, D)) * sx),
            "weight": bf(np.random.standard_normal((O, C, 1, S)) / C ** 0.25 / s.T[None, :, None, :])}


def reference(x, weight):
    xp = f64(x).reshape(B, C, D // (S0 + 1), S0 + 1).sum(axis=-1)
    xr = xp.reshape(B, C, P, S)
    a = xr.transpose(0, 2, 3, 1).reshape(B, P, K)
    w = f64(weight)[:, :, 0, :].transpose(2, 1, 0).reshape(K, O)
    out = (mxq(a, 2, "e4m3") @ mxq(w, 0, "e4m3")) / np.sqrt(C)
    return out.transpose(0, 2, 1)

@@ -1,0 +1,89 @@
+from contextlib import ExitStack
+
+import concourse.mybir as mybir
+from concourse.masks import make_identity
+
+BF16 = mybir.dt.bfloat16
+F32 = mybir.dt.float32
+U32 = mybir.dt.uint32
+U8 = mybir.dt.uint8
+FP8X4 = mybir.dt.float8_e4m3fn_x4
+
+B, C, D, O = 2, 256, 2048, 128
+TAPS = 2
+PAIR = 2
+POSITIONS = D // (TAPS * PAIR)
+PARTS = 128
+CH = C // PARTS
+PACK = CH * TAPS
+N_CHUNK = 256
+CHUNKS = POSITIONS // N_CHUNK
+FLOPS = 2 * B * O * POSITIONS * C * TAPS
+
+
+def tile_nonoverlappingconv1d_shared_s_kernel(tc, x, weight, out):
+    nc = tc.nc
+    with ExitStack() as ctx:
+        keep = ctx.enter_context(tc.tile_pool(name="keep", bufs=1))
+        stream = ctx.enter_context(tc.tile_pool(name="stream", bufs=B * CHUNKS))
+        psum_w = ctx.enter_context(tc.psum_pool(name="psum_w", bufs=1))
+        psum_acc = ctx.enter_context(tc.psum_pool(name="psum_acc", bufs=B * CHUNKS))
+
+        w_rows = keep.tile([O, C * TAPS], BF16)
+        nc.scalar.dma_start(out=w_rows[:], in_=weight.rearrange("o c one k -> o (c one k)"))
+
+        raws = []
+        for b in range(B):
+            x_rows = x[b].rearrange("(q e) d -> q e d", e=CH)
+            for h in range(CHUNKS):
+                width = N_CHUNK * TAPS * PAIR
+                raw = stream.tile([PARTS, CH, width], BF16, name="raw")
+                nc.sync.dma_start(out=raw[:], in_=x_rows[:, :, h * width : (h + 1) * width])
+                raws.append(raw)
+
+        identity = keep.tile([PARTS, PARTS], F32)
+        make_identity(nc, identity[:])
+        w_words = w_rows[:].bitcast(F32)
+        w_turned = psum_w.tile([PARTS, CH, O], F32)
+        for e in range(CH):
+            nc.tensor.transpose(w_turned[:, e, :], w_words[:, e : C : CH], identity[:])
+        w_grouped = keep.tile([PARTS, O * PACK], BF16, align_bytes=64)
+        nc.scalar.copy(
+            out=w_grouped[:].bitcast(F32).rearrange("q (o e) -> q o e", e=CH),
+            in_=w_turned[:].rearrange("q e o -> q o e"),
+        )
+        w_codes = keep.tile([PARTS, O], U32, align_bytes=64)
+        w_scales = keep.tile([PARTS, O], U8, align_bytes=64)
+        nc.vector.quantize_mx(out=w_codes[:].bitcast(FP8X4), scales=w_scales[:], in_=w_grouped[:])
+
+        for b in range(B):
+            for h in range(CHUNKS):
+                raw = raws[b * CHUNKS + h]
+                pairs = raw[:].rearrange("q e (p k s) -> q p e k s", k=TAPS, s=PAIR)
+                x_grouped = stream.tile([PARTS, N_CHUNK * PACK], BF16, align_bytes=64)
+                nc.vector.tensor_tensor(
+                    out=x_grouped[:].rearrange("q (p e k) -> q p e k", e=CH, k=TAPS),
+                    in0=pairs[:, :, :, :, 0],
+                    in1=pairs[:, :, :, :, 1],
+                    op=mybir.AluOpType.add,
+                )
+                x_codes = stream.tile([PARTS, N_CHUNK], U32, align_bytes=64)
+                x_scales = stream.tile([PARTS, N_CHUNK], U8, align_bytes=64)
+                nc.vector.quantize_mx(
+                    out=x_codes[:].bitcast(FP8X4), scales=x_scales[:], in_=x_grouped[:]
+                )
+                acc = psum_acc.tile([O, N_CHUNK], F32)
+                nc.tensor.matmul_mx(
+                    out=acc[:],
+                    lhsT=w_codes[:].bitcast(FP8X4),
+                    lhsT_scale=w_scales[:],
+                    rhs=x_codes[:].bitcast(FP8X4),
+                    rhs_scale=x_scales[:],
+                    start=True,
+                    stop=True,
+                )
+                result = stream.tile([O, N_CHUNK], F32)
+                nc.scalar.mul(out=result[:], in_=acc[:], mul=1.0 / 16.0)
+                nc.sync.dma_start(
+                    out=out[b, :, h * N_CHUNK : (h + 1) * N_CHUNK], in_=result[:]
+                )

@@ -16,30 +16,40 @@ POSITIONS = D // (TAPS * PAIR)
 PARTS = 128
 CH = C // PARTS
 PACK = CH * TAPS
-N_CHUNK = 256
-CHUNKS = POSITIONS // N_CHUNK
+N_NARROW = 128
+N_WIDE = 256
+RISING = (N_NARROW, N_NARROW, N_WIDE)
 FLOPS = 2 * B * O * POSITIONS * C * TAPS
 
 
 def tile_nonoverlappingconv1d_shared_s_kernel(tc, x, weight, out):
     nc = tc.nc
+    assert B == 2 and sum(RISING) == POSITIONS
+    chunks = []
+    for b, widths in enumerate((RISING, tuple(reversed(RISING)))):
+        first = 0
+        for n in widths:
+            chunks.append((b, first, n))
+            first += n
+    count = len(chunks)
+
     with ExitStack() as ctx:
+        ctx.enter_context(tc.manual_schedule())
         keep = ctx.enter_context(tc.tile_pool(name="keep", bufs=1))
-        stream = ctx.enter_context(tc.tile_pool(name="stream", bufs=B * CHUNKS))
+        stream = ctx.enter_context(tc.tile_pool(name="stream", bufs=count))
         psum_w = ctx.enter_context(tc.psum_pool(name="psum_w", bufs=1))
-        psum_acc = ctx.enter_context(tc.psum_pool(name="psum_acc", bufs=B * CHUNKS))
+        psum_acc = ctx.enter_context(tc.psum_pool(name="psum_acc", bufs=count))
 
         w_rows = keep.tile([O, C * TAPS], BF16)
         nc.scalar.dma_start(out=w_rows[:], in_=weight.rearrange("o c one k -> o (c one k)"))
 
         raws = []
-        for b in range(B):
+        for b, first, n in chunks:
             x_rows = x[b].rearrange("(q e) d -> q e d", e=CH)
-            for h in range(CHUNKS):
-                width = N_CHUNK * TAPS * PAIR
-                raw = stream.tile([PARTS, CH, width], BF16, name="raw")
-                nc.sync.dma_start(out=raw[:], in_=x_rows[:, :, h * width : (h + 1) * width])
-                raws.append(raw)
+            span = TAPS * PAIR
+            raw = stream.tile([PARTS, CH, n * span], BF16, name="raw")
+            nc.sync.dma_start(out=raw[:], in_=x_rows[:, :, first * span : (first + n) * span])
+            raws.append(raw)
 
         identity = keep.tile([PARTS, PARTS], F32)
         make_identity(nc, identity[:])
@@ -54,36 +64,55 @@ def tile_nonoverlappingconv1d_shared_s_kernel(tc, x, weight, out):
         )
         w_codes = keep.tile([PARTS, O], U32, align_bytes=64)
         w_scales = keep.tile([PARTS, O], U8, align_bytes=64)
-        nc.vector.quantize_mx(out=w_codes[:].bitcast(FP8X4), scales=w_scales[:], in_=w_grouped[:])
 
-        for b in range(B):
-            for h in range(CHUNKS):
-                raw = raws[b * CHUNKS + h]
-                pairs = raw[:].rearrange("q e (p k s) -> q p e k s", k=TAPS, s=PAIR)
-                x_grouped = stream.tile([PARTS, N_CHUNK * PACK], BF16, align_bytes=64)
-                nc.vector.tensor_tensor(
-                    out=x_grouped[:].rearrange("q (p e k) -> q p e k", e=CH, k=TAPS),
-                    in0=pairs[:, :, :, :, 0],
-                    in1=pairs[:, :, :, :, 1],
-                    op=mybir.AluOpType.add,
-                )
-                x_codes = stream.tile([PARTS, N_CHUNK], U32, align_bytes=64)
-                x_scales = stream.tile([PARTS, N_CHUNK], U8, align_bytes=64)
+        grouped = []
+        codes = []
+        scales = []
+
+        def sum_pairs(i):
+            n = chunks[i][2]
+            pairs = raws[i][:].rearrange("q e (p k s) -> q p e k s", k=TAPS, s=PAIR)
+            x_grouped = stream.tile([PARTS, n * PACK], BF16, align_bytes=64, name="x_grouped")
+            nc.vector.tensor_tensor(
+                out=x_grouped[:].rearrange("q (p e k) -> q p e k", e=CH, k=TAPS),
+                in0=pairs[:, :, :, :, 0],
+                in1=pairs[:, :, :, :, 1],
+                op=mybir.AluOpType.add,
+            )
+            grouped.append(x_grouped)
+
+        def quantise(i):
+            n = chunks[i][2]
+            x_codes = stream.tile([PARTS, n], U32, align_bytes=64, name="x_codes")
+            x_scales = stream.tile([PARTS, n], U8, align_bytes=64, name="x_scales")
+            nc.vector.quantize_mx(
+                out=x_codes[:].bitcast(FP8X4), scales=x_scales[:], in_=grouped[i][:]
+            )
+            codes.append(x_codes)
+            scales.append(x_scales)
+
+        sum_pairs(0)
+        for i in range(count):
+            if i + 1 < count:
+                sum_pairs(i + 1)
+            if chunks[i][0] == 1 and chunks[i][1] == 0:
                 nc.vector.quantize_mx(
-                    out=x_codes[:].bitcast(FP8X4), scales=x_scales[:], in_=x_grouped[:]
+                    out=w_codes[:].bitcast(FP8X4), scales=w_scales[:], in_=w_grouped[:]
                 )
-                acc = psum_acc.tile([O, N_CHUNK], F32)
-                nc.tensor.matmul_mx(
-                    out=acc[:],
-                    lhsT=w_codes[:].bitcast(FP8X4),
-                    lhsT_scale=w_scales[:],
-                    rhs=x_codes[:].bitcast(FP8X4),
-                    rhs_scale=x_scales[:],
-                    start=True,
-                    stop=True,
-                )
-                result = stream.tile([O, N_CHUNK], F32)
-                nc.scalar.mul(out=result[:], in_=acc[:], mul=1.0 / 16.0)
-                nc.sync.dma_start(
-                    out=out[b, :, h * N_CHUNK : (h + 1) * N_CHUNK], in_=result[:]
-                )
+            quantise(i)
+
+        for i in range(count):
+            b, first, n = chunks[i]
+            acc = psum_acc.tile([O, n], F32, name="acc")
+            nc.tensor.matmul_mx(
+                out=acc[:],
+                lhsT=w_codes[:].bitcast(FP8X4),
+                lhsT_scale=w_scales[:],
+                rhs=codes[i][:].bitcast(FP8X4),
+                rhs_scale=scales[i][:],
+                start=True,
+                stop=True,
+            )
+            result = stream.tile([O, n], F32, name="result")
+            nc.scalar.mul(out=result[:], in_=acc[:], mul=1.0 / 16.0)
+            nc.sync.dma_start(out=out[b, :, first : first + n], in_=result[:])

@@ -16,9 +16,8 @@ POSITIONS = D // (TAPS * PAIR)
 PARTS = 128
 CH = C // PARTS
 PACK = CH * TAPS
-N_NARROW = 128
-N_WIDE = 256
-RISING = (N_NARROW, N_NARROW, N_WIDE)
+RISING = (64, 64, 128, 256)
+PSUM_BANKS = 8
 FLOPS = 2 * B * O * POSITIONS * C * TAPS
 
 
@@ -38,13 +37,13 @@ def tile_nonoverlappingconv1d_shared_s_kernel(tc, x, weight, out):
         keep = ctx.enter_context(tc.tile_pool(name="keep", bufs=1))
         stream = ctx.enter_context(tc.tile_pool(name="stream", bufs=count))
         psum_w = ctx.enter_context(tc.psum_pool(name="psum_w", bufs=1))
-        psum_acc = ctx.enter_context(tc.psum_pool(name="psum_acc", bufs=count))
+        psum_acc = ctx.enter_context(tc.psum_pool(name="psum_acc", bufs=PSUM_BANKS - 1))
 
         w_rows = keep.tile([O, C * TAPS], BF16)
-        nc.scalar.dma_start(out=w_rows[:], in_=weight.rearrange("o c one k -> o (c one k)"))
-
         raws = []
         for b, first, n in chunks:
+            if b == 1 and first == 0:
+                nc.sync.dma_start(out=w_rows[:], in_=weight.rearrange("o c one k -> o (c one k)"))
             x_rows = x[b].rearrange("(q e) d -> q e d", e=CH)
             span = TAPS * PAIR
             raw = stream.tile([PARTS, CH, n * span], BF16, name="raw")

@@ -16,8 +16,9 @@ POSITIONS = D // (TAPS * PAIR)
 PARTS = 128
 CH = C // PARTS
 PACK = CH * TAPS
-RISING = (64, 64, 128, 256)
-PSUM_BANKS = 8
+N_NARROW = 128
+N_WIDE = 256
+RISING = (N_NARROW, N_NARROW, N_WIDE)
 FLOPS = 2 * B * O * POSITIONS * C * TAPS
 
 
@@ -37,7 +38,7 @@ def tile_nonoverlappingconv1d_shared_s_kernel(tc, x, weight, out):
         keep = ctx.enter_context(tc.tile_pool(name="keep", bufs=1))
         stream = ctx.enter_context(tc.tile_pool(name="stream", bufs=count))
         psum_w = ctx.enter_context(tc.psum_pool(name="psum_w", bufs=1))
-        psum_acc = ctx.enter_context(tc.psum_pool(name="psum_acc", bufs=PSUM_BANKS - 1))
+        psum_acc = ctx.enter_context(tc.psum_pool(name="psum_acc", bufs=count))
 
         w_rows = keep.tile([O, C * TAPS], BF16)
         raws = []

from contextlib import ExitStack

import concourse.mybir as mybir
from concourse.masks import make_identity

BF16 = mybir.dt.bfloat16
F32 = mybir.dt.float32
U32 = mybir.dt.uint32
U8 = mybir.dt.uint8
FP8X4 = mybir.dt.float8_e4m3fn_x4

B, C, D, O = 2, 256, 2048, 128
TAPS = 2
PAIR = 2
POSITIONS = D // (TAPS * PAIR)
PARTS = 128
CH = C // PARTS
PACK = CH * TAPS
N_NARROW = 128
N_WIDE = 256
RISING = (N_NARROW, N_NARROW, N_WIDE)
FLOPS = 2 * B * O * POSITIONS * C * TAPS


def tile_nonoverlappingconv1d_shared_s_kernel(tc, x, weight, out):
    nc = tc.nc
    assert B == 2 and sum(RISING) == POSITIONS
    chunks = []
    for b, widths in enumerate((RISING, tuple(reversed(RISING)))):
        first = 0
        for n in widths:
            chunks.append((b, first, n))
            first += n
    count = len(chunks)

    with ExitStack() as ctx:
        ctx.enter_context(tc.manual_schedule())
        keep = ctx.enter_context(tc.tile_pool(name="keep", bufs=1))
        stream = ctx.enter_context(tc.tile_pool(name="stream", bufs=count))
        psum_w = ctx.enter_context(tc.psum_pool(name="psum_w", bufs=1))
        psum_acc = ctx.enter_context(tc.psum_pool(name="psum_acc", bufs=count))

        w_rows = keep.tile([O, C * TAPS], BF16)
        raws = []
        for b, first, n in chunks:
            if b == 1 and first == 0:
                nc.sync.dma_start(out=w_rows[:], in_=weight.rearrange("o c one k -> o (c one k)"))
            x_rows = x[b].rearrange("(q e) d -> q e d", e=CH)
            span = TAPS * PAIR
            raw = stream.tile([PARTS, CH, n * span], BF16, name="raw")
            nc.sync.dma_start(out=raw[:], in_=x_rows[:, :, first * span : (first + n) * span])
            raws.append(raw)

        identity = keep.tile([PARTS, PARTS], F32)
        make_identity(nc, identity[:])
        w_words = w_rows[:].bitcast(F32)
        w_turned = psum_w.tile([PARTS, CH, O], F32)
        for e in range(CH):
            nc.tensor.transpose(w_turned[:, e, :], w_words[:, e : C : CH], identity[:])
        w_grouped = keep.tile([PARTS, O * PACK], BF16, align_bytes=64)
        nc.scalar.copy(
            out=w_grouped[:].bitcast(F32).rearrange("q (o e) -> q o e", e=CH),
            in_=w_turned[:].rearrange("q e o -> q o e"),
        )
        w_codes = keep.tile([PARTS, O], U32, align_bytes=64)
        w_scales = keep.tile([PARTS, O], U8, align_bytes=64)

        grouped = []
        codes = []
        scales = []

        def sum_pairs(i):
            n = chunks[i][2]
            pairs = raws[i][:].rearrange("q e (p k s) -> q p e k s", k=TAPS, s=PAIR)
            x_grouped = stream.tile([PARTS, n * PACK], BF16, align_bytes=64, name="x_grouped")
            nc.vector.tensor_tensor(
                out=x_grouped[:].rearrange("q (p e k) -> q p e k", e=CH, k=TAPS),
                in0=pairs[:, :, :, :, 0],
                in1=pairs[:, :, :, :, 1],
                op=mybir.AluOpType.add,
            )
            grouped.append(x_grouped)

        def quantise(i):
            n = chunks[i][2]
            x_codes = stream.tile([PARTS, n], U32, align_bytes=64, name="x_codes")
            x_scales = stream.tile([PARTS, n], U8, align_bytes=64, name="x_scales")
            nc.vector.quantize_mx(
                out=x_codes[:].bitcast(FP8X4), scales=x_scales[:], in_=grouped[i][:]
            )
            codes.append(x_codes)
            scales.append(x_scales)

        sum_pairs(0)
        for i in range(count):
            if i + 1 < count:
                sum_pairs(i + 1)
            if chunks[i][0] == 1 and chunks[i][1] == 0:
                nc.vector.quantize_mx(
                    out=w_codes[:].bitcast(FP8X4), scales=w_scales[:], in_=w_grouped[:]
                )
            quantise(i)

        for i in range(count):
            b, first, n = chunks[i]
            acc = psum_acc.tile([O, n], F32, name="acc")
            nc.tensor.matmul_mx(
                out=acc[:],
                lhsT=w_codes[:].bitcast(FP8X4),
                lhsT_scale=w_scales[:],
                rhs=codes[i][:].bitcast(FP8X4),
                rhs_scale=scales[i][:],
                start=True,
                stop=True,
            )
            result = stream.tile([O, n], F32, name="result")
            nc.scalar.mul(out=result[:], in_=acc[:], mul=1.0 / 16.0)
            nc.sync.dma_start(out=out[b, :, first : first + n], in_=result[:])
